import numpy as np
import ml_dtypes


def mxq(x, axis, fmt="e4m3"):
    dtype, down = {"e4m3": (ml_dtypes.float8_e4m3fn, 7), "e5m2": (ml_dtypes.float8_e5m2, 14)}[fmt]
    v = np.moveaxis(np.asarray(x, np.float32).astype(ml_dtypes.bfloat16).astype(np.float64), axis, -1)
    blocks = v.reshape(v.shape[:-1] + (-1, 32))
    amax = np.abs(blocks).max(-1, keepdims=True)
    byte = np.maximum(np.where(amax > 0, np.frexp(amax)[1] - 1 + 127, 0) - down, 1)
    scale = np.exp2(byte - 127.0)
    codes = (blocks / scale).astype(np.float32).astype(dtype).astype(np.float64)
    return np.moveaxis((codes * scale).reshape(v.shape), -1, axis)


WIDE = False


def mx_kscale(k):
    if not WIDE:
        return np.ones(k)
    levels = np.array([10, -10, 5, -5, 0])
    if k % 512:
        return np.exp2(np.random.permutation(np.resize(levels, k // 32))).repeat(32)
    a = np.empty((k // 512, 16))
    for p in range(k // 512):
        a[p, :8] = np.random.permutation(np.resize(levels, 8))
        for g in range(8):
            far = levels[np.abs(levels - a[p, g]) >= 10]
            a[p, g + 8] = far[np.random.randint(len(far))]
    return np.exp2(a.ravel()).repeat(32)


BF16 = ml_dtypes.bfloat16


def bf(x):
    return np.asarray(x, np.float32).astype(BF16)


def f64(x):
    return np.asarray(x).astype(np.float64)


B, L, F, D, N = 128, 32, 512, 1024, 8192
TOP = 0.8 * np.sqrt(2.0 * np.log(L))


def elu(v):
    return np.where(v > 0.0, v, np.exp(np.minimum(v, 0.0)) - 1.0)


def setup_inputs():
    s = mx_kscale(F)
    return {"x": bf(np.random.standard_normal((B, L, F)) * s),
            "conv_w": bf(np.random.standard_normal((D, F)) / np.sqrt(F) / s),
            "conv_b": bf(np.random.standard_normal(D) * 2.0 - TOP)}


def reference(x, conv_w, conv_b):
    z = (mxq(f64(x), 2, "e4m3") @ mxq(f64(conv_w), 1, "e4m3").T) + f64(conv_b)
    return elu(z).max(axis=1)

@@ -1,0 +1,187 @@
+from contextlib import ExitStack
+
+import concourse.mybir as mybir
+from concourse.masks import make_identity
+
+F32 = mybir.dt.float32
+BF16 = mybir.dt.bfloat16
+U32 = mybir.dt.uint32
+U8 = mybir.dt.uint8
+I32 = mybir.dt.int32
+FP8X4 = mybir.dt.float8_e4m3fn_x4
+ALU = mybir.AluOpType
+ACT = mybir.ActivationFunctionType
+
+P = 128
+SEQS, POSITIONS, FEATURES, CHANNELS = 128, 32, 512, 1024
+WORDS = FEATURES // 2
+PAIR = 2
+PAIR_COLS = PAIR * P
+HALF = 512
+HALVES = CHANNELS // HALF
+AHEAD = 2
+WARM_UP = 6
+PIECES = 2
+CHAINS = 2
+
+FLOPS = 2 * SEQS * POSITIONS * FEATURES * CHANNELS
+
+
+def tile_conceptembedmodel_pa_kernel(tc, x, conv_w, conv_b, out):
+    nc = tc.nc
+    with ExitStack() as ctx:
+        keep = ctx.enter_context(tc.tile_pool(name="keep", bufs=1))
+        stage = ctx.enter_context(tc.tile_pool(name="stage", bufs=AHEAD + 2))
+        running = ctx.enter_context(tc.tile_pool(name="running", bufs=2))
+        finish_pool = ctx.enter_context(tc.tile_pool(name="finish", bufs=2))
+        turn_pool = ctx.enter_context(tc.psum_pool(name="turn", bufs=3))
+        z_pool = ctx.enter_context(tc.psum_pool(name="z", bufs=5))
+        ctx.enter_context(tc.manual_schedule())
+
+        ident = keep.tile([P, P], F32)
+        make_identity(nc, ident[:])
+
+        zeros = keep.tile([P, HALF], BF16)
+        nc.vector.memset(zeros[:].bitcast(I32), 0)
+
+        def idle_matmul():
+            unread = z_pool.tile([P, HALF], F32, tag="z")
+            nc.tensor.matmul(out=unread[:], lhsT=zeros[:, :P], rhs=zeros[:], start=True, stop=True)
+
+        for i in range(WARM_UP):
+            idle_matmul()
+
+        x_raw = keep.tile([P, POSITIONS * FEATURES], BF16)
+        w_raw = keep.tile([P, (CHANNELS // P) * FEATURES], BF16)
+        bias = keep.tile([P, CHANNELS], BF16)
+        raw_cols = PAIR * FEATURES
+
+        def load_w_pair(j):
+            nc.sync.dma_start(
+                out=w_raw[:, j * raw_cols : (j + 1) * raw_cols].rearrange(
+                    "r (s f) -> r s f", s=PAIR
+                ),
+                in_=conv_w[j * PAIR_COLS : (j + 1) * PAIR_COLS, :].rearrange(
+                    "(s r) f -> r s f", s=PAIR
+                ),
+            )
+
+        def load_x_pair(j):
+            nc.sync.dma_start(
+                out=x_raw[:, j * raw_cols : (j + 1) * raw_cols],
+                in_=x[:, j * PAIR : (j + 1) * PAIR, :].rearrange("b l f -> b (l f)"),
+            )
+
+        pairs_per_half = HALF // PAIR_COLS
+        for j in range(pairs_per_half):
+            load_w_pair(j)
+        for j in range(POSITIONS // PAIR):
+            load_x_pair(j)
+        for j in range(pairs_per_half, HALVES * pairs_per_half):
+            load_w_pair(j)
+        nc.sync.dma_start(out=bias[:], in_=conv_b.partition_broadcast(P))
+
+        x_codes = keep.tile([P, POSITIONS * P], U32, align_bytes=64)
+        x_scales = keep.tile([P, POSITIONS * P], U8, align_bytes=64)
+        w_codes = keep.tile([P, CHANNELS], U32, align_bytes=64)
+        w_scales = keep.tile([P, CHANNELS], U8, align_bytes=64)
+        x_words = x_raw[:].bitcast(F32)
+        w_words = w_raw[:].bitcast(F32)
+
+        def turn_pair(words, j):
+            turned = turn_pool.tile([P, PAIR, 2, P], F32)
+            for s in range(PAIR):
+                for u in range(2):
+                    first = (j * PAIR + s) * WORDS
+                    nc.tensor.transpose(
+                        turned[:, s, u, :], words[:, first + u : first + WORDS : 2], ident[:]
+                    )
+            grouped = stage.tile([P, PAIR_COLS * 4], BF16, align_bytes=64)
+            nc.scalar.copy(
+                out=grouped[:].bitcast(F32).rearrange("p (s r u) -> p s r u", s=PAIR, u=2),
+                in_=turned[:].rearrange("p s u r -> p s r u"),
+            )
+            return grouped
+
+        def quantise_pair(grouped, codes, scales, j):
+            cols = slice(j * PAIR_COLS, (j + 1) * PAIR_COLS)
+            nc.vector.quantize_mx(
+                out=codes[:, cols].bitcast(FP8X4), scales=scales[:, cols], in_=grouped[:]
+            )
+
+        def new_maxima():
+            return [running.tile([P, HALF], F32, name="best%d" % c) for c in range(CHAINS)]
+
+        def multiply_and_fold(h, l, best):
+            z = z_pool.tile([P, HALF], F32)
+            seqs = slice(l * P, (l + 1) * P)
+            chans = slice(h * HALF, (h + 1) * HALF)
+            nc.tensor.matmul_mx(
+                out=z[:],
+                lhsT=x_codes[:, seqs].bitcast(FP8X4),
+                lhsT_scale=x_scales[:, seqs],
+                rhs=w_codes[:, chans].bitcast(FP8X4),
+                rhs_scale=w_scales[:, chans],
+                start=True,
+                stop=True,
+            )
+            chain = best[l % CHAINS]
+            if l < CHAINS:
+                nc.scalar.copy(out=chain[:], in_=z[:])
+            else:
+                nc.vector.tensor_tensor(out=chain[:], in0=z[:], in1=chain[:], op=ALU.max)
+
+        def finish_half(h, best, engine):
+            chans = slice(h * HALF, (h + 1) * HALF)
+            top = finish_pool.tile([P, HALF], F32)
+            nc.vector.tensor_tensor(out=top[:], in0=best[0][:], in1=best[1][:], op=ALU.max)
+            v = finish_pool.tile([P, HALF], F32)
+            engine.tensor_tensor(out=v[:], in0=top[:], in1=bias[:, chans], op=ALU.add)
+            below = finish_pool.tile([P, HALF], F32)
+            grown = finish_pool.tile([P, HALF], F32)
+            above = finish_pool.tile([P, HALF], F32)
+            result = finish_pool.tile([P, HALF], F32)
+            width = HALF // PIECES
+            pieces = [slice(c * width, (c + 1) * width) for c in range(PIECES)]
+            for piece in pieces:
+                engine.tensor_scalar(
+                    out=below[:, piece], in0=v[:, piece], scalar1=0.0, scalar2=None, op0=ALU.min
+                )
+                nc.scalar.activation(out=grown[:, piece], in_=below[:, piece], func=ACT.Exp)
+            engine.tensor_scalar(
+                out=above[:], in0=v[:], scalar1=0.0, scalar2=-1.0, op0=ALU.max, op1=ALU.add
+            )
+            for c in range(PIECES):
+                piece = pieces[c]
+                engine.tensor_tensor(
+                    out=result[:, piece], in0=above[:, piece], in1=grown[:, piece], op=ALU.add
+                )
+                first = h * HALF + c * width
+                nc.sync.dma_start(out=out[:, first : first + width], in_=result[:, piece])
+
+        x_pairs = POSITIONS // PAIR
+        to_prepare = [(w_words, w_codes, w_scales, j) for j in range(pairs_per_half)]
+        to_prepare += [(x_words, x_codes, x_scales, j) for j in range(x_pairs)]
+        to_prepare += [
+            (w_words, w_codes, w_scales, j) for j in range(pairs_per_half, HALVES * pairs_per_half)
+        ]
+        started = pairs_per_half + AHEAD
+        for words, codes, scales, i in to_prepare[:started]:
+            quantise_pair(turn_pair(words, i), codes, scales, i)
+            idle_matmul()
+        best_first = new_maxima()
+        for j in range(x_pairs):
+            coming = to_prepare[started + j : started + j + 1]
+            regrouped = [turn_pair(words, i) for words, codes, scales, i in coming]
+            for l in range(j * PAIR, (j + 1) * PAIR):
+                multiply_and_fold(0, l, best_first)
+            for grouped, (words, codes, scales, i) in zip(regrouped, coming):
+                quantise_pair(grouped, codes, scales, i)
+
+        best_second = new_maxima()
+        for l in range(CHAINS):
+            multiply_and_fold(1, l, best_second)
+        finish_half(0, best_first, nc.gpsimd)
+        for l in range(CHAINS, POSITIONS):
+            multiply_and_fold(1, l, best_second)
+        finish_half(1, best_second, nc.vector)

@@ -17,25 +17,35 @@ SEQS, POSITIONS, FEATURES, CHANNELS = 128, 32, 512, 1024
 WORDS = FEATURES // 2
 PAIR = 2
 PAIR_COLS = PAIR * P
+PAIR_VALUES = PAIR_COLS * 4
 HALF = 512
-HALVES = CHANNELS // HALF
-AHEAD = 2
+GROUP = 4
+GROUPS = POSITIONS // GROUP
+PAIRS = GROUP // PAIR
+W_PAIRS = HALF // PAIR_COLS
 WARM_UP = 6
 PIECES = 2
-CHAINS = 2
 
 FLOPS = 2 * SEQS * POSITIONS * FEATURES * CHANNELS
+
+
+def joined(h, g):
+    return g < GROUPS - 1 and (h, g) != (0, 0)
+
+
+def negated(g):
+    return joined(1, g)
 
 
 def tile_conceptembedmodel_pa_kernel(tc, x, conv_w, conv_b, out):
     nc = tc.nc
     with ExitStack() as ctx:
         keep = ctx.enter_context(tc.tile_pool(name="keep", bufs=1))
-        stage = ctx.enter_context(tc.tile_pool(name="stage", bufs=AHEAD + 2))
-        running = ctx.enter_context(tc.tile_pool(name="running", bufs=2))
+        stage = ctx.enter_context(tc.tile_pool(name="stage", bufs=4))
+        parts = ctx.enter_context(tc.tile_pool(name="parts", bufs=2))
         finish_pool = ctx.enter_context(tc.tile_pool(name="finish", bufs=2))
-        turn_pool = ctx.enter_context(tc.psum_pool(name="turn", bufs=3))
-        z_pool = ctx.enter_context(tc.psum_pool(name="z", bufs=5))
+        turn_pool = ctx.enter_context(tc.psum_pool(name="turn", bufs=2))
+        z_pool = ctx.enter_context(tc.psum_pool(name="z", bufs=6))
         ctx.enter_context(tc.manual_schedule())
 
         ident = keep.tile([P, P], F32)
@@ -43,42 +53,38 @@ def tile_conceptembedmodel_pa_kernel(tc, x, conv_w, conv_b, out):
 
         zeros = keep.tile([P, HALF], BF16)
         nc.vector.memset(zeros[:].bitcast(I32), 0)
-
-        def idle_matmul():
+        for i in range(WARM_UP):
             unread = z_pool.tile([P, HALF], F32, tag="z")
             nc.tensor.matmul(out=unread[:], lhsT=zeros[:, :P], rhs=zeros[:], start=True, stop=True)
-
-        for i in range(WARM_UP):
-            idle_matmul()
 
         x_raw = keep.tile([P, POSITIONS * FEATURES], BF16)
         w_raw = keep.tile([P, (CHANNELS // P) * FEATURES], BF16)
         bias = keep.tile([P, CHANNELS], BF16)
         raw_cols = PAIR * FEATURES
 
-        def load_w_pair(j):
-            nc.sync.dma_start(
-                out=w_raw[:, j * raw_cols : (j + 1) * raw_cols].rearrange(
-                    "r (s f) -> r s f", s=PAIR
-                ),
-                in_=conv_w[j * PAIR_COLS : (j + 1) * PAIR_COLS, :].rearrange(
-                    "(s r) f -> r s f", s=PAIR
-                ),
-            )
+        def load_w_half(h):
+            for j in range(h * W_PAIRS, (h + 1) * W_PAIRS):
+                nc.sync.dma_start(
+                    out=w_raw[:, j * raw_cols : (j + 1) * raw_cols].rearrange(
+                        "r (s f) -> r s f", s=PAIR
+                    ),
+                    in_=conv_w[j * PAIR_COLS : (j + 1) * PAIR_COLS, :].rearrange(
+                        "(s r) f -> r s f", s=PAIR
+                    ),
+                )
 
-        def load_x_pair(j):
-            nc.sync.dma_start(
-                out=x_raw[:, j * raw_cols : (j + 1) * raw_cols],
-                in_=x[:, j * PAIR : (j + 1) * PAIR, :].rearrange("b l f -> b (l f)"),
-            )
+        def load_x_group(g):
+            for j in range(g * PAIRS, (g + 1) * PAIRS):
+                nc.sync.dma_start(
+                    out=x_raw[:, j * raw_cols : (j + 1) * raw_cols],
+                    in_=x[:, j * PAIR : (j + 1) * PAIR, :].rearrange("b l f -> b (l f)"),
+                )
 
-        pairs_per_half = HALF // PAIR_COLS
-        for j in range(pairs_per_half):
-            load_w_pair(j)
-        for j in range(POSITIONS // PAIR):
-            load_x_pair(j)
-        for j in range(pairs_per_half, HALVES * pairs_per_half):
-            load_w_pair(j)
+        load_w_half(0)
+        load_x_group(0)
+        load_w_half(1)
+        for g in range(1, GROUPS):
+            load_x_group(g)
         nc.sync.dma_start(out=bias[:], in_=conv_b.partition_broadcast(P))
 
         x_codes = keep.tile([P, POSITIONS * P], U32, align_bytes=64)
@@ -88,100 +94,220 @@ def tile_conceptembedmodel_pa_kernel(tc, x, conv_w, conv_b, out):
         x_words = x_raw[:].bitcast(F32)
         w_words = w_raw[:].bitcast(F32)
 
-        def turn_pair(words, j):
-            turned = turn_pool.tile([P, PAIR, 2, P], F32)
+        def turn_pair(words, j, pool, tag):
+            turned = pool.tile([P, PAIR, 2, P], F32, tag=tag)
             for s in range(PAIR):
                 for u in range(2):
                     first = (j * PAIR + s) * WORDS
                     nc.tensor.transpose(
                         turned[:, s, u, :], words[:, first + u : first + WORDS : 2], ident[:]
                     )
-            grouped = stage.tile([P, PAIR_COLS * 4], BF16, align_bytes=64)
-            nc.scalar.copy(
-                out=grouped[:].bitcast(F32).rearrange("p (s r u) -> p s r u", s=PAIR, u=2),
-                in_=turned[:].rearrange("p s u r -> p s r u"),
-            )
-            return grouped
+            return turned
 
-        def quantise_pair(grouped, codes, scales, j):
-            cols = slice(j * PAIR_COLS, (j + 1) * PAIR_COLS)
+        def new_values(pairs):
+            values = stage.tile([P, pairs * PAIR_VALUES], BF16, tag="v%d" % pairs, align_bytes=64)
+            return values
+
+        def regroup(turned, values, copy, flip=None):
+            if flip is None:
+                copy(
+                    out=values.bitcast(F32).rearrange("p (s r u) -> p s r u", s=PAIR, u=2),
+                    in_=turned[:].rearrange("p s u r -> p s r u"),
+                )
+                return
+            for s in range(PAIR):
+                block = values[:, s * P * 4 : (s + 1) * P * 4]
+                if s == flip:
+                    nc.scalar.activation(
+                        out=block.rearrange("p (r u e) -> p r u e", u=2, e=2),
+                        in_=turned[:, s, :, :]
+                        .rearrange("p u r -> p (u r)")
+                        .bitcast(BF16)
+                        .rearrange("p (u r e) -> p r u e", u=2, e=2),
+                        func=ACT.Copy,
+                        scale=-1.0,
+                    )
+                else:
+                    copy(
+                        out=block.bitcast(F32).rearrange("p (r u) -> p r u", u=2),
+                        in_=turned[:, s, :, :].rearrange("p u r -> p r u"),
+                    )
+
+        def quantise(values, codes, scales, j, pairs):
+            cols = slice(j * PAIR_COLS, (j + pairs) * PAIR_COLS)
             nc.vector.quantize_mx(
-                out=codes[:, cols].bitcast(FP8X4), scales=scales[:, cols], in_=grouped[:]
+                out=codes[:, cols].bitcast(FP8X4), scales=scales[:, cols], in_=values
             )
 
-        def new_maxima():
-            return [running.tile([P, HALF], F32, name="best%d" % c) for c in range(CHAINS)]
+        def prepare_group(g):
+            turned = [turn_pair(x_words, g * PAIRS + k, turn_pool, "turn") for k in range(PAIRS)]
+            values = new_values(PAIRS)
+            regroup(turned[0], values[:, :PAIR_VALUES], nc.scalar.copy, 1 if negated(g) else None)
+            regroup(turned[1], values[:, PAIR_VALUES:], nc.scalar.copy)
+            return values
 
-        def multiply_and_fold(h, l, best):
+        def multiply(h, *positions):
             z = z_pool.tile([P, HALF], F32)
-            seqs = slice(l * P, (l + 1) * P)
             chans = slice(h * HALF, (h + 1) * HALF)
-            nc.tensor.matmul_mx(
-                out=z[:],
-                lhsT=x_codes[:, seqs].bitcast(FP8X4),
-                lhsT_scale=x_scales[:, seqs],
-                rhs=w_codes[:, chans].bitcast(FP8X4),
-                rhs_scale=w_scales[:, chans],
-                start=True,
-                stop=True,
-            )
-            chain = best[l % CHAINS]
-            if l < CHAINS:
-                nc.scalar.copy(out=chain[:], in_=z[:])
-            else:
-                nc.vector.tensor_tensor(out=chain[:], in0=z[:], in1=chain[:], op=ALU.max)
+            for k, l in enumerate(positions):
+                seqs = slice(l * P, (l + 1) * P)
+                nc.tensor.matmul_mx(
+                    out=z[:],
+                    lhsT=x_codes[:, seqs].bitcast(FP8X4),
+                    lhsT_scale=x_scales[:, seqs],
+                    rhs=w_codes[:, chans].bitcast(FP8X4),
+                    rhs_scale=w_scales[:, chans],
+                    start=(k == 0),
+                    stop=(k == len(positions) - 1),
+                )
+            return z
 
-        def finish_half(h, best, engine):
-            chans = slice(h * HALF, (h + 1) * HALF)
-            top = finish_pool.tile([P, HALF], F32)
-            nc.vector.tensor_tensor(out=top[:], in0=best[0][:], in1=best[1][:], op=ALU.max)
+        best = keep.tile([P, CHANNELS], F32)
+        larger = keep.tile([P, CHANNELS], F32)
+
+        def columns(h):
+            return slice(h * HALF, (h + 1) * HALF)
+
+        def fold(h, z):
+            cols = columns(h)
+            nc.vector.tensor_tensor(out=best[:, cols], in0=z[:], in1=best[:, cols], op=ALU.max)
+
+        def start(h, z):
+            nc.scalar.copy(out=best[:, columns(h)], in_=z[:])
+
+        def finish_first_half():
             v = finish_pool.tile([P, HALF], F32)
-            engine.tensor_tensor(out=v[:], in0=top[:], in1=bias[:, chans], op=ALU.add)
+            above = finish_pool.tile([P, HALF], F32)
             below = finish_pool.tile([P, HALF], F32)
             grown = finish_pool.tile([P, HALF], F32)
+            less = finish_pool.tile([P, HALF], F32)
+            result = finish_pool.tile([P, HALF], F32)
+            cols = columns(0)
+            nc.gpsimd.tensor_tensor(out=v[:], in0=best[:, cols], in1=bias[:, cols], op=ALU.add)
+            nc.scalar.activation(out=below[:], in_=v[:], func=ACT.Relu, scale=-1.0)
+            nc.scalar.activation(out=grown[:], in_=below[:], func=ACT.Exp, scale=-1.0)
+            nc.scalar.add(out=less[:], in_=grown[:], add=-1.0)
+            nc.scalar.activation(out=above[:], in_=v[:], func=ACT.Relu)
+            nc.gpsimd.tensor_tensor(out=result[:], in0=above[:], in1=less[:], op=ALU.add)
+            nc.sync.dma_start(out=out[:, cols], in_=result[:])
+
+        def finish_second_half(last):
+            v = finish_pool.tile([P, HALF], F32)
             above = finish_pool.tile([P, HALF], F32)
+            below = finish_pool.tile([P, HALF], F32)
+            grown = finish_pool.tile([P, HALF], F32)
             result = finish_pool.tile([P, HALF], F32)
             width = HALF // PIECES
             pieces = [slice(c * width, (c + 1) * width) for c in range(PIECES)]
-            for piece in pieces:
-                engine.tensor_scalar(
+            wide = [slice(HALF + c * width, HALF + (c + 1) * width) for c in range(PIECES)]
+            for piece, cols in zip(pieces, wide):
+                nc.vector.tensor_tensor(
+                    out=best[:, cols], in0=last[:, piece], in1=best[:, cols], op=ALU.max
+                )
+                nc.vector.tensor_tensor(
+                    out=v[:, piece], in0=best[:, cols], in1=bias[:, cols], op=ALU.add
+                )
+                nc.vector.tensor_scalar(
                     out=below[:, piece], in0=v[:, piece], scalar1=0.0, scalar2=None, op0=ALU.min
                 )
                 nc.scalar.activation(out=grown[:, piece], in_=below[:, piece], func=ACT.Exp)
-            engine.tensor_scalar(
-                out=above[:], in0=v[:], scalar1=0.0, scalar2=-1.0, op0=ALU.max, op1=ALU.add
-            )
-            for c in range(PIECES):
-                piece = pieces[c]
-                engine.tensor_tensor(
+            for piece in pieces:
+                nc.vector.tensor_scalar(
+                    out=above[:, piece],
+                    in0=v[:, piece],
+                    scalar1=0.0,
+                    scalar2=-1.0,
+                    op0=ALU.max,
+                    op1=ALU.add,
+                )
+            for piece, cols in zip(pieces, wide):
+                nc.vector.tensor_tensor(
                     out=result[:, piece], in0=above[:, piece], in1=grown[:, piece], op=ALU.add
                 )
-                first = h * HALF + c * width
-                nc.sync.dma_start(out=out[:, first : first + width], in_=result[:, piece])
+                nc.sync.dma_start(out=out[:, cols], in_=result[:, piece])
 
-        x_pairs = POSITIONS // PAIR
-        to_prepare = [(w_words, w_codes, w_scales, j) for j in range(pairs_per_half)]
-        to_prepare += [(x_words, x_codes, x_scales, j) for j in range(x_pairs)]
-        to_prepare += [
-            (w_words, w_codes, w_scales, j) for j in range(pairs_per_half, HALVES * pairs_per_half)
-        ]
-        started = pairs_per_half + AHEAD
-        for words, codes, scales, i in to_prepare[:started]:
-            quantise_pair(turn_pair(words, i), codes, scales, i)
-            idle_matmul()
-        best_first = new_maxima()
-        for j in range(x_pairs):
-            coming = to_prepare[started + j : started + j + 1]
-            regrouped = [turn_pair(words, i) for words, codes, scales, i in coming]
-            for l in range(j * PAIR, (j + 1) * PAIR):
-                multiply_and_fold(0, l, best_first)
-            for grouped, (words, codes, scales, i) in zip(regrouped, coming):
-                quantise_pair(grouped, codes, scales, i)
+        turned_w = [turn_pair(w_words, j, turn_pool, "turn") for j in range(W_PAIRS)]
+        turned_x = [turn_pair(x_words, j, z_pool, "z") for j in range(PAIRS)]
+        w_values = [new_values(1) for j in range(W_PAIRS)]
+        x_values = [new_values(1) for j in range(PAIRS)]
+        regroup(turned_w[0], w_values[0][:], nc.scalar.copy)
+        regroup(turned_w[1], w_values[1][:], nc.vector.tensor_copy)
+        regroup(turned_x[0], x_values[0][:], nc.scalar.copy, 1 if negated(0) else None)
+        regroup(turned_x[1], x_values[1][:], nc.scalar.copy)
+        for j in range(W_PAIRS):
+            quantise(w_values[j][:], w_codes, w_scales, j, 1)
+        quantise(x_values[0][:], x_codes, x_scales, 0, 1)
+        turned_w = [turn_pair(w_words, W_PAIRS + j, turn_pool, "turn") for j in range(W_PAIRS)]
+        w_values = new_values(W_PAIRS)
+        regroup(turned_w[0], w_values[:, :PAIR_VALUES], nc.vector.tensor_copy)
+        regroup(turned_w[1], w_values[:, PAIR_VALUES:], nc.scalar.copy)
+        quantise(x_values[1][:], x_codes, x_scales, 1, 1)
+        start(0, multiply(0, 0))
+        opposite = multiply(0, 1)
+        nc.vector.scalar_tensor_tensor(
+            out=best[:, columns(0)],
+            in0=opposite[:],
+            scalar=-1.0,
+            in1=best[:, columns(0)],
+            op0=ALU.mult,
+            op1=ALU.max,
+        )
+        quantise(w_values[:], w_codes, w_scales, W_PAIRS, W_PAIRS)
+        coming = prepare_group(1)
+        fold(0, multiply(0, 2))
+        fold(0, multiply(0, 3))
+        quantise(coming[:], x_codes, x_scales, PAIRS, PAIRS)
 
-        best_second = new_maxima()
-        for l in range(CHAINS):
-            multiply_and_fold(1, l, best_second)
-        finish_half(0, best_first, nc.gpsimd)
-        for l in range(CHAINS, POSITIONS):
-            multiply_and_fold(1, l, best_second)
-        finish_half(1, best_second, nc.vector)
+        waiting = None
+        for i in range(1, GROUPS + 1):
+            work = [(h, i - h) for h in (1, 0) if i - h < GROUPS]
+            coming = prepare_group(i + 1) if i < GROUPS - 1 else None
+
+            due = waiting
+            if due is not None:
+                cols, base, gain = due
+                nc.gpsimd.tensor_tensor(
+                    out=larger[:, cols], in0=base[:, cols], in1=gain[:, cols], op=ALU.add
+                )
+            if i == GROUPS:
+                finish_first_half()
+            waiting = None
+            halves = [h for h, g in work if joined(h, g)]
+            if halves:
+                base = parts.tile([P, CHANNELS], F32)
+                gain = parts.tile([P, CHANNELS], F32)
+                waiting = (slice(halves[-1] * HALF, (halves[0] + 1) * HALF), base, gain)
+
+            for h, g in work:
+                z = multiply(h, g * GROUP + 2)
+                if (h, g) == (1, 0):
+                    start(h, z)
+                else:
+                    fold(h, z)
+            for h, g in work:
+                if joined(h, g):
+                    nc.scalar.copy(out=base[:, columns(h)], in_=multiply(h, g * GROUP)[:])
+                    nc.scalar.activation(
+                        out=gain[:, columns(h)],
+                        in_=multiply(h, g * GROUP, g * GROUP + 1)[:],
+                        func=ACT.Relu,
+                        scale=-1.0,
+                    )
+                else:
+                    fold(h, multiply(h, g * GROUP))
+
+            if coming is not None:
+                quantise(coming[:], x_codes, x_scales, (i + 1) * PAIRS, PAIRS)
+            if due is not None:
+                cols = due[0]
+                nc.vector.tensor_tensor(
+                    out=best[:, cols], in0=larger[:, cols], in1=best[:, cols], op=ALU.max
+                )
+            for h, g in work:
+                if not joined(h, g):
+                    fold(h, multiply(h, g * GROUP + 1))
+            for h, g in work:
+                last = multiply(h, g * GROUP + 3)
+                if i < GROUPS:
+                    fold(h, last)
+        finish_second_half(last)

@@ -23,18 +23,10 @@ GROUP = 4
 GROUPS = POSITIONS // GROUP
 PAIRS = GROUP // PAIR
 W_PAIRS = HALF // PAIR_COLS
-WARM_UP = 6
+WARM_UP = 5
 PIECES = 2
 
 FLOPS = 2 * SEQS * POSITIONS * FEATURES * CHANNELS
-
-
-def joined(h, g):
-    return g < GROUPS - 1 and (h, g) != (0, 0)
-
-
-def negated(g):
-    return joined(1, g)
 
 
 def tile_conceptembedmodel_pa_kernel(tc, x, conv_w, conv_b, out):
@@ -43,7 +35,7 @@ def tile_conceptembedmodel_pa_kernel(tc, x, conv_w, conv_b, out):
         keep = ctx.enter_context(tc.tile_pool(name="keep", bufs=1))
         stage = ctx.enter_context(tc.tile_pool(name="stage", bufs=4))
         parts = ctx.enter_context(tc.tile_pool(name="parts", bufs=2))
-        finish_pool = ctx.enter_context(tc.tile_pool(name="finish", bufs=2))
+        finish_pool = ctx.enter_context(tc.tile_pool(name="finish", bufs=1))
         turn_pool = ctx.enter_context(tc.psum_pool(name="turn", bufs=2))
         z_pool = ctx.enter_context(tc.psum_pool(name="z", bufs=6))
         ctx.enter_context(tc.manual_schedule())
@@ -53,9 +45,14 @@ def tile_conceptembedmodel_pa_kernel(tc, x, conv_w, conv_b, out):
 
         zeros = keep.tile([P, HALF], BF16)
         nc.vector.memset(zeros[:].bitcast(I32), 0)
-        for i in range(WARM_UP):
-            unread = z_pool.tile([P, HALF], F32, tag="z")
+
+        unread = z_pool.tile([P, HALF], F32, tag="z")
+
+        def idle_matmul():
             nc.tensor.matmul(out=unread[:], lhsT=zeros[:, :P], rhs=zeros[:], start=True, stop=True)
+
+        for i in range(WARM_UP):
+            idle_matmul()
 
         x_raw = keep.tile([P, POSITIONS * FEATURES], BF16)
         w_raw = keep.tile([P, (CHANNELS // P) * FEATURES], BF16)
@@ -82,8 +79,9 @@ def tile_conceptembedmodel_pa_kernel(tc, x, conv_w, conv_b, out):
 
         load_w_half(0)
         load_x_group(0)
+        load_x_group(1)
         load_w_half(1)
-        for g in range(1, GROUPS):
+        for g in range(2, GROUPS):
             load_x_group(g)
         nc.sync.dma_start(out=bias[:], in_=conv_b.partition_broadcast(P))
 
@@ -142,8 +140,8 @@ def tile_conceptembedmodel_pa_kernel(tc, x, conv_w, conv_b, out):
         def prepare_group(g):
             turned = [turn_pair(x_words, g * PAIRS + k, turn_pool, "turn") for k in range(PAIRS)]
             values = new_values(PAIRS)
-            regroup(turned[0], values[:, :PAIR_VALUES], nc.scalar.copy, 1 if negated(g) else None)
-            regroup(turned[1], values[:, PAIR_VALUES:], nc.scalar.copy)
+            regroup(turned[0], values[:, :PAIR_VALUES], nc.scalar.copy)
+            regroup(turned[1], values[:, PAIR_VALUES:], nc.scalar.copy, 1 if g < GROUPS - 1 else None)
             return values
 
         def multiply(h, *positions):
@@ -168,146 +166,168 @@ def tile_conceptembedmodel_pa_kernel(tc, x, conv_w, conv_b, out):
         def columns(h):
             return slice(h * HALF, (h + 1) * HALF)
 
-        def fold(h, z):
-            cols = columns(h)
-            nc.vector.tensor_tensor(out=best[:, cols], in0=z[:], in1=best[:, cols], op=ALU.max)
+        def fold(h, z, pieces=1):
+            width = HALF // pieces
+            for c in range(pieces):
+                cols = slice(h * HALF + c * width, h * HALF + (c + 1) * width)
+                nc.vector.tensor_tensor(
+                    out=best[:, cols],
+                    in0=z[:, c * width : (c + 1) * width],
+                    in1=best[:, cols],
+                    op=ALU.max,
+                )
 
         def start(h, z):
             nc.scalar.copy(out=best[:, columns(h)], in_=z[:])
 
-        def finish_first_half():
-            v = finish_pool.tile([P, HALF], F32)
-            above = finish_pool.tile([P, HALF], F32)
-            below = finish_pool.tile([P, HALF], F32)
-            grown = finish_pool.tile([P, HALF], F32)
-            less = finish_pool.tile([P, HALF], F32)
-            result = finish_pool.tile([P, HALF], F32)
-            cols = columns(0)
-            nc.gpsimd.tensor_tensor(out=v[:], in0=best[:, cols], in1=bias[:, cols], op=ALU.add)
-            nc.scalar.activation(out=below[:], in_=v[:], func=ACT.Relu, scale=-1.0)
-            nc.scalar.activation(out=grown[:], in_=below[:], func=ACT.Exp, scale=-1.0)
-            nc.scalar.add(out=less[:], in_=grown[:], add=-1.0)
-            nc.scalar.activation(out=above[:], in_=v[:], func=ACT.Relu)
-            nc.gpsimd.tensor_tensor(out=result[:], in0=above[:], in1=less[:], op=ALU.add)
-            nc.sync.dma_start(out=out[:, cols], in_=result[:])
+        def fold_opposite(h, z):
+            cols = columns(h)
+            nc.vector.scalar_tensor_tensor(
+                out=best[:, cols],
+                in0=z[:],
+                scalar=-1.0,
+                in1=best[:, cols],
+                op0=ALU.mult,
+                op1=ALU.max,
+            )
 
-        def finish_second_half(last):
-            v = finish_pool.tile([P, HALF], F32)
-            above = finish_pool.tile([P, HALF], F32)
-            below = finish_pool.tile([P, HALF], F32)
-            grown = finish_pool.tile([P, HALF], F32)
-            result = finish_pool.tile([P, HALF], F32)
+        def join(h, g, base, gain):
+            c, d = g * GROUP + 2, g * GROUP + 3
+            cols = columns(h)
+            nc.scalar.copy(out=base[:, cols], in_=multiply(h, c)[:])
+            nc.scalar.activation(
+                out=gain[:, cols], in_=multiply(h, c, d)[:], func=ACT.Relu, scale=-1.0
+            )
+
+        def add_joined(halves, base, gain):
+            cols = slice(halves[0] * HALF, (halves[-1] + 1) * HALF)
+            nc.gpsimd.tensor_tensor(
+                out=larger[:, cols], in0=base[:, cols], in1=gain[:, cols], op=ALU.add
+            )
+
+        finish_tiles = [finish_pool.tile([P, CHANNELS], F32, name="f%d" % k) for k in range(5)]
+        v, above, below, grown, result = finish_tiles
+
+        def finish_first_half():
+            cols = columns(0)
+            nc.gpsimd.tensor_tensor(
+                out=v[:, cols], in0=best[:, cols], in1=bias[:, cols], op=ALU.add
+            )
+            nc.scalar.activation(out=below[:, cols], in_=v[:, cols], func=ACT.Relu, scale=-1.0)
+            nc.scalar.activation(out=above[:, cols], in_=v[:, cols], func=ACT.Relu)
+            nc.scalar.activation(out=grown[:, cols], in_=below[:, cols], func=ACT.Exp, scale=-1.0)
+
+        def store(cols):
+            nc.vector.scalar_tensor_tensor(
+                out=result[:, cols],
+                in0=grown[:, cols],
+                scalar=-1.0,
+                in1=above[:, cols],
+                op0=ALU.add,
+                op1=ALU.add,
+            )
+            nc.sync.dma_start(out=out[:, cols], in_=result[:, cols])
+
+        def finish_second_half():
             width = HALF // PIECES
-            pieces = [slice(c * width, (c + 1) * width) for c in range(PIECES)]
-            wide = [slice(HALF + c * width, HALF + (c + 1) * width) for c in range(PIECES)]
-            for piece, cols in zip(pieces, wide):
+            pieces = [slice(HALF + c * width, HALF + (c + 1) * width) for c in range(PIECES)]
+            for cols in pieces:
                 nc.vector.tensor_tensor(
-                    out=best[:, cols], in0=last[:, piece], in1=best[:, cols], op=ALU.max
+                    out=v[:, cols], in0=best[:, cols], in1=bias[:, cols], op=ALU.add
                 )
-                nc.vector.tensor_tensor(
-                    out=v[:, piece], in0=best[:, cols], in1=bias[:, cols], op=ALU.add
-                )
+            for cols in pieces:
                 nc.vector.tensor_scalar(
-                    out=below[:, piece], in0=v[:, piece], scalar1=0.0, scalar2=None, op0=ALU.min
+                    out=below[:, cols], in0=v[:, cols], scalar1=0.0, scalar2=None, op0=ALU.min
                 )
-                nc.scalar.activation(out=grown[:, piece], in_=below[:, piece], func=ACT.Exp)
-            for piece in pieces:
-                nc.vector.tensor_scalar(
-                    out=above[:, piece],
-                    in0=v[:, piece],
-                    scalar1=0.0,
-                    scalar2=-1.0,
-                    op0=ALU.max,
-                    op1=ALU.add,
-                )
-            for piece, cols in zip(pieces, wide):
-                nc.vector.tensor_tensor(
-                    out=result[:, piece], in0=above[:, piece], in1=grown[:, piece], op=ALU.add
-                )
-                nc.sync.dma_start(out=out[:, cols], in_=result[:, piece])
+                nc.scalar.activation(out=grown[:, cols], in_=below[:, cols], func=ACT.Exp)
+            cols = columns(1)
+            nc.vector.tensor_scalar(
+                out=above[:, cols], in0=v[:, cols], scalar1=0.0, scalar2=None, op0=ALU.max
+            )
+            store(columns(0))
+            for cols in pieces:
+                store(cols)
 
         turned_w = [turn_pair(w_words, j, turn_pool, "turn") for j in range(W_PAIRS)]
         turned_x = [turn_pair(x_words, j, z_pool, "z") for j in range(PAIRS)]
+        idle_matmul()
         w_values = [new_values(1) for j in range(W_PAIRS)]
         x_values = [new_values(1) for j in range(PAIRS)]
+        next_values = new_values(PAIRS)
         regroup(turned_w[0], w_values[0][:], nc.scalar.copy)
         regroup(turned_w[1], w_values[1][:], nc.vector.tensor_copy)
-        regroup(turned_x[0], x_values[0][:], nc.scalar.copy, 1 if negated(0) else None)
-        regroup(turned_x[1], x_values[1][:], nc.scalar.copy)
+        regroup(turned_x[0], x_values[0][:], nc.scalar.copy)
+        regroup(turned_x[1], x_values[1][:], nc.scalar.copy, 1)
         for j in range(W_PAIRS):
             quantise(w_values[j][:], w_codes, w_scales, j, 1)
         quantise(x_values[0][:], x_codes, x_scales, 0, 1)
-        turned_w = [turn_pair(w_words, W_PAIRS + j, turn_pool, "turn") for j in range(W_PAIRS)]
+        turned_x = [turn_pair(x_words, PAIRS, turn_pool, "turn")]
+        idle_matmul()
+        regroup(turned_x[0], next_values[:, :PAIR_VALUES], nc.vector.tensor_copy)
+        start(0, multiply(0, 0))
+        second = multiply(0, 1)
+        quantise(x_values[1][:], x_codes, x_scales, 1, 1)
+        turned_x.append(turn_pair(x_words, PAIRS + 1, turn_pool, "turn"))
+        turned_w = [turn_pair(w_words, W_PAIRS + j, z_pool, "z") for j in range(W_PAIRS)]
         w_values = new_values(W_PAIRS)
         regroup(turned_w[0], w_values[:, :PAIR_VALUES], nc.vector.tensor_copy)
+        fold(0, second)
+        regroup(turned_x[1], next_values[:, PAIR_VALUES:], nc.scalar.copy, 1)
+        third, opposite = multiply(0, 2), multiply(0, 3)
         regroup(turned_w[1], w_values[:, PAIR_VALUES:], nc.scalar.copy)
-        quantise(x_values[1][:], x_codes, x_scales, 1, 1)
-        start(0, multiply(0, 0))
-        opposite = multiply(0, 1)
-        nc.vector.scalar_tensor_tensor(
-            out=best[:, columns(0)],
-            in0=opposite[:],
-            scalar=-1.0,
-            in1=best[:, columns(0)],
-            op0=ALU.mult,
-            op1=ALU.max,
-        )
+        quantise(next_values[:], x_codes, x_scales, PAIRS, PAIRS)
+        fold(0, third)
         quantise(w_values[:], w_codes, w_scales, W_PAIRS, W_PAIRS)
-        coming = prepare_group(1)
-        fold(0, multiply(0, 2))
-        fold(0, multiply(0, 3))
-        quantise(coming[:], x_codes, x_scales, PAIRS, PAIRS)
+        fold_opposite(0, opposite)
 
-        waiting = None
-        for i in range(1, GROUPS + 1):
-            work = [(h, i - h) for h in (1, 0) if i - h < GROUPS]
-            coming = prepare_group(i + 1) if i < GROUPS - 1 else None
+        def new_parts():
+            base = parts.tile([P, CHANNELS], F32)
+            gain = parts.tile([P, CHANNELS], F32)
+            return base, gain
 
-            due = waiting
-            if due is not None:
-                cols, base, gain = due
-                nc.gpsimd.tensor_tensor(
-                    out=larger[:, cols], in0=base[:, cols], in1=gain[:, cols], op=ALU.add
-                )
-            if i == GROUPS:
-                finish_first_half()
-            waiting = None
-            halves = [h for h, g in work if joined(h, g)]
-            if halves:
-                base = parts.tile([P, CHANNELS], F32)
-                gain = parts.tile([P, CHANNELS], F32)
-                waiting = (slice(halves[-1] * HALF, (halves[0] + 1) * HALF), base, gain)
+        base, gain = new_parts()
+        coming = prepare_group(2)
+        fold(0, multiply(0, GROUP))
+        start(1, multiply(1, 0))
+        join(0, 1, base, gain)
+        waiting = [0]
+        fold(1, multiply(1, 1))
+        quantise(coming[:], x_codes, x_scales, 2 * PAIRS, PAIRS)
+        fold_opposite(1, multiply(1, 3))
+        fold(0, multiply(0, GROUP + 1))
+        fold(1, multiply(1, 2))
 
+        for i in range(2, GROUPS - 1):
+            coming = prepare_group(i + 1)
+            add_joined(waiting, base, gain)
+            base, gain = new_parts()
+            work = [(0, i), (1, i - 1)]
             for h, g in work:
-                z = multiply(h, g * GROUP + 2)
-                if (h, g) == (1, 0):
-                    start(h, z)
-                else:
-                    fold(h, z)
+                fold(h, multiply(h, g * GROUP))
             for h, g in work:
-                if joined(h, g):
-                    nc.scalar.copy(out=base[:, columns(h)], in_=multiply(h, g * GROUP)[:])
-                    nc.scalar.activation(
-                        out=gain[:, columns(h)],
-                        in_=multiply(h, g * GROUP, g * GROUP + 1)[:],
-                        func=ACT.Relu,
-                        scale=-1.0,
-                    )
-                else:
-                    fold(h, multiply(h, g * GROUP))
+                join(h, g, base, gain)
+            quantise(coming[:], x_codes, x_scales, (i + 1) * PAIRS, PAIRS)
+            for h in waiting:
+                fold(h, larger[:, columns(h)])
+            for h, g in work:
+                fold(h, multiply(h, g * GROUP + 1))
+            waiting = [0, 1]
 
-            if coming is not None:
-                quantise(coming[:], x_codes, x_scales, (i + 1) * PAIRS, PAIRS)
-            if due is not None:
-                cols = due[0]
-                nc.vector.tensor_tensor(
-                    out=best[:, cols], in0=larger[:, cols], in1=best[:, cols], op=ALU.max
-                )
-            for h, g in work:
-                if not joined(h, g):
-                    fold(h, multiply(h, g * GROUP + 1))
-            for h, g in work:
-                last = multiply(h, g * GROUP + 3)
-                if i < GROUPS:
-                    fold(h, last)
-        finish_second_half(last)
+        last = GROUPS - 1
+        add_joined(waiting, base, gain)
+        base, gain = new_parts()
+        fold(0, multiply(0, last * GROUP))
+        fold(1, multiply(1, (last - 1) * GROUP))
+        join(1, last - 1, base, gain)
+        fold(0, multiply(0, last * GROUP + 1))
+        fold(1, multiply(1, (last - 1) * GROUP + 1))
+        fold(0, larger[:, columns(0)])
+        fold(1, larger[:, columns(1)])
+        fold(0, multiply(0, last * GROUP + 2), PIECES)
+        fold(0, multiply(0, last * GROUP + 3), PIECES)
+        add_joined([1], base, gain)
+        finish_first_half()
+        for l in range(GROUP):
+            fold(1, multiply(1, last * GROUP + l), PIECES)
+        fold(1, larger[:, columns(1)], PIECES)
+        finish_second_half()

@@ -161,7 +161,7 @@ def tile_conceptembedmodel_pa_kernel(tc, x, conv_w, conv_b, out):
             return z
 
         best = keep.tile([P, CHANNELS], F32)
-        larger = keep.tile([P, CHANNELS], F32)
+        larger = keep.tile([P, 3 * HALF], F32)
 
         def columns(h):
             return slice(h * HALF, (h + 1) * HALF)
@@ -191,18 +191,36 @@ def tile_conceptembedmodel_pa_kernel(tc, x, conv_w, conv_b, out):
                 op1=ALU.max,
             )
 
-        def join(h, g, base, gain):
+        def place(h, i):
+            third = 1 if h == 0 else 2 * (i % 2)
+            return slice(third * HALF, (third + 1) * HALF)
+
+        def inside(h, i):
+            first = place(h, i).start - (i % 2) * HALF
+            return slice(first, first + HALF)
+
+        def new_parts():
+            base = parts.tile([P, CHANNELS], F32)
+            gain = parts.tile([P, CHANNELS], F32)
+            return base, gain
+
+        def join(h, g, i, base, gain):
             c, d = g * GROUP + 2, g * GROUP + 3
-            cols = columns(h)
+            cols = inside(h, i)
             nc.scalar.copy(out=base[:, cols], in_=multiply(h, c)[:])
             nc.scalar.activation(
                 out=gain[:, cols], in_=multiply(h, c, d)[:], func=ACT.Relu, scale=-1.0
             )
 
-        def add_joined(halves, base, gain):
-            cols = slice(halves[0] * HALF, (halves[-1] + 1) * HALF)
+        def add_joined(halves, i, base, gain):
+            starts = [inside(h, i).start for h in halves]
+            cols = slice(min(starts), max(starts) + HALF)
+            shift = (i % 2) * HALF
             nc.gpsimd.tensor_tensor(
-                out=larger[:, cols], in0=base[:, cols], in1=gain[:, cols], op=ALU.add
+                out=larger[:, cols.start + shift : cols.stop + shift],
+                in0=base[:, cols],
+                in1=gain[:, cols],
+                op=ALU.add,
             )
 
         finish_tiles = [finish_pool.tile([P, CHANNELS], F32, name="f%d" % k) for k in range(5)]
@@ -280,16 +298,11 @@ def tile_conceptembedmodel_pa_kernel(tc, x, conv_w, conv_b, out):
         quantise(w_values[:], w_codes, w_scales, W_PAIRS, W_PAIRS)
         fold_opposite(0, opposite)
 
-        def new_parts():
-            base = parts.tile([P, CHANNELS], F32)
-            gain = parts.tile([P, CHANNELS], F32)
-            return base, gain
-
-        base, gain = new_parts()
         coming = prepare_group(2)
         fold(0, multiply(0, GROUP))
         start(1, multiply(1, 0))
-        join(0, 1, base, gain)
+        base, gain = new_parts()
+        join(0, 1, 1, base, gain)
         waiting = [0]
         fold(1, multiply(1, 1))
         quantise(coming[:], x_codes, x_scales, 2 * PAIRS, PAIRS)
@@ -299,35 +312,35 @@ def tile_conceptembedmodel_pa_kernel(tc, x, conv_w, conv_b, out):
 
         for i in range(2, GROUPS - 1):
             coming = prepare_group(i + 1)
-            add_joined(waiting, base, gain)
+            add_joined(waiting, i - 1, base, gain)
             base, gain = new_parts()
             work = [(0, i), (1, i - 1)]
             for h, g in work:
                 fold(h, multiply(h, g * GROUP))
             for h, g in work:
-                join(h, g, base, gain)
+                join(h, g, i, base, gain)
             quantise(coming[:], x_codes, x_scales, (i + 1) * PAIRS, PAIRS)
             for h in waiting:
-                fold(h, larger[:, columns(h)])
+                fold(h, larger[:, place(h, i - 1)])
             for h, g in work:
                 fold(h, multiply(h, g * GROUP + 1))
             waiting = [0, 1]
 
         last = GROUPS - 1
-        add_joined(waiting, base, gain)
+        add_joined(waiting, last - 1, base, gain)
         base, gain = new_parts()
         fold(0, multiply(0, last * GROUP))
         fold(1, multiply(1, (last - 1) * GROUP))
-        join(1, last - 1, base, gain)
+        join(1, last - 1, last, base, gain)
         fold(0, multiply(0, last * GROUP + 1))
         fold(1, multiply(1, (last - 1) * GROUP + 1))
-        fold(0, larger[:, columns(0)])
-        fold(1, larger[:, columns(1)])
+        fold(0, larger[:, place(0, last - 1)])
+        fold(1, larger[:, place(1, last - 1)])
         fold(0, multiply(0, last * GROUP + 2), PIECES)
         fold(0, multiply(0, last * GROUP + 3), PIECES)
-        add_joined([1], base, gain)
+        add_joined([1], last, base, gain)
         finish_first_half()
         for l in range(GROUP):
             fold(1, multiply(1, last * GROUP + l), PIECES)
-        fold(1, larger[:, columns(1)], PIECES)
+        fold(1, larger[:, place(1, last)], PIECES)
         finish_second_half()

@@ -59,28 +59,33 @@ def tile_conceptembedmodel_pa_kernel(tc, x, conv_w, conv_b, out):
         bias = keep.tile([P, CHANNELS], BF16)
         raw_cols = PAIR * FEATURES
 
-        def load_w_half(h):
-            for j in range(h * W_PAIRS, (h + 1) * W_PAIRS):
-                nc.sync.dma_start(
-                    out=w_raw[:, j * raw_cols : (j + 1) * raw_cols].rearrange(
-                        "r (s f) -> r s f", s=PAIR
-                    ),
-                    in_=conv_w[j * PAIR_COLS : (j + 1) * PAIR_COLS, :].rearrange(
-                        "(s r) f -> r s f", s=PAIR
-                    ),
-                )
+        def load_w_pair(j):
+            nc.sync.dma_start(
+                out=w_raw[:, j * raw_cols : (j + 1) * raw_cols].rearrange(
+                    "r (s f) -> r s f", s=PAIR
+                ),
+                in_=conv_w[j * PAIR_COLS : (j + 1) * PAIR_COLS, :].rearrange(
+                    "(s r) f -> r s f", s=PAIR
+                ),
+            )
+
+        def load_x_pair(j):
+            nc.sync.dma_start(
+                out=x_raw[:, j * raw_cols : (j + 1) * raw_cols],
+                in_=x[:, j * PAIR : (j + 1) * PAIR, :].rearrange("b l f -> b (l f)"),
+            )
 
         def load_x_group(g):
             for j in range(g * PAIRS, (g + 1) * PAIRS):
-                nc.sync.dma_start(
-                    out=x_raw[:, j * raw_cols : (j + 1) * raw_cols],
-                    in_=x[:, j * PAIR : (j + 1) * PAIR, :].rearrange("b l f -> b (l f)"),
-                )
+                load_x_pair(j)
 
-        load_w_half(0)
-        load_x_group(0)
+        load_w_pair(0)
+        load_x_pair(0)
+        load_w_pair(1)
+        load_x_pair(1)
         load_x_group(1)
-        load_w_half(1)
+        load_w_pair(2)
+        load_w_pair(3)
         for g in range(2, GROUPS):
             load_x_group(g)
         nc.sync.dma_start(out=bias[:], in_=conv_b.partition_broadcast(P))
@@ -144,13 +149,13 @@ def tile_conceptembedmodel_pa_kernel(tc, x, conv_w, conv_b, out):
             regroup(turned[1], values[:, PAIR_VALUES:], nc.scalar.copy, 1 if g < GROUPS - 1 else None)
             return values
 
-        def multiply(h, *positions):
+        def multiply(h, *positions, part=slice(0, HALF)):
             z = z_pool.tile([P, HALF], F32)
-            chans = slice(h * HALF, (h + 1) * HALF)
+            chans = slice(h * HALF + part.start, h * HALF + part.stop)
             for k, l in enumerate(positions):
                 seqs = slice(l * P, (l + 1) * P)
                 nc.tensor.matmul_mx(
-                    out=z[:],
+                    out=z[:, part],
                     lhsT=x_codes[:, seqs].bitcast(FP8X4),
                     lhsT_scale=x_scales[:, seqs],
                     rhs=w_codes[:, chans].bitcast(FP8X4),
@@ -177,8 +182,9 @@ def tile_conceptembedmodel_pa_kernel(tc, x, conv_w, conv_b, out):
                     op=ALU.max,
                 )
 
-        def start(h, z):
-            nc.scalar.copy(out=best[:, columns(h)], in_=z[:])
+        def start(h, z, part=slice(0, HALF)):
+            cols = slice(h * HALF + part.start, h * HALF + part.stop)
+            nc.scalar.copy(out=best[:, cols], in_=z[:, part])
 
         def fold_opposite(h, z):
             cols = columns(h)
@@ -266,32 +272,40 @@ def tile_conceptembedmodel_pa_kernel(tc, x, conv_w, conv_b, out):
             for cols in pieces:
                 store(cols)
 
-        turned_w = [turn_pair(w_words, j, turn_pool, "turn") for j in range(W_PAIRS)]
-        turned_x = [turn_pair(x_words, j, z_pool, "z") for j in range(PAIRS)]
-        idle_matmul()
+        parts_w = [slice(j * PAIR_COLS, (j + 1) * PAIR_COLS) for j in range(W_PAIRS)]
         w_values = [new_values(1) for j in range(W_PAIRS)]
         x_values = [new_values(1) for j in range(PAIRS)]
         next_values = new_values(PAIRS)
+        turned_w = [turn_pair(w_words, 0, turn_pool, "turn")]
+        turned_x = [turn_pair(x_words, 0, z_pool, "z")]
+        turned_w.append(turn_pair(w_words, 1, turn_pool, "turn"))
+        turned_x.append(turn_pair(x_words, 1, z_pool, "z"))
+        idle_matmul()
         regroup(turned_w[0], w_values[0][:], nc.scalar.copy)
-        regroup(turned_w[1], w_values[1][:], nc.vector.tensor_copy)
-        regroup(turned_x[0], x_values[0][:], nc.scalar.copy)
+        regroup(turned_x[0], x_values[0][:], nc.vector.tensor_copy)
+        regroup(turned_w[1], w_values[1][:], nc.scalar.copy)
         regroup(turned_x[1], x_values[1][:], nc.scalar.copy, 1)
-        for j in range(W_PAIRS):
-            quantise(w_values[j][:], w_codes, w_scales, j, 1)
+        quantise(w_values[0][:], w_codes, w_scales, 0, 1)
         quantise(x_values[0][:], x_codes, x_scales, 0, 1)
         turned_x = [turn_pair(x_words, PAIRS, turn_pool, "turn")]
-        idle_matmul()
+        start(0, multiply(0, 0, part=parts_w[0]), parts_w[0])
+        second = [multiply(0, 1, part=parts_w[0])]
+        quantise(w_values[1][:], w_codes, w_scales, 1, 1)
         regroup(turned_x[0], next_values[:, :PAIR_VALUES], nc.vector.tensor_copy)
-        start(0, multiply(0, 0))
-        second = multiply(0, 1)
-        quantise(x_values[1][:], x_codes, x_scales, 1, 1)
+        start(0, multiply(0, 0, part=parts_w[1]), parts_w[1])
+        second.append(multiply(0, 1, part=parts_w[1]))
         turned_x.append(turn_pair(x_words, PAIRS + 1, turn_pool, "turn"))
+        quantise(x_values[1][:], x_codes, x_scales, 1, 1)
+        for k in range(W_PAIRS):
+            cols = parts_w[k]
+            nc.vector.tensor_tensor(
+                out=best[:, cols], in0=second[k][:, cols], in1=best[:, cols], op=ALU.max
+            )
         turned_w = [turn_pair(w_words, W_PAIRS + j, z_pool, "z") for j in range(W_PAIRS)]
         w_values = new_values(W_PAIRS)
-        regroup(turned_w[0], w_values[:, :PAIR_VALUES], nc.vector.tensor_copy)
-        fold(0, second)
         regroup(turned_x[1], next_values[:, PAIR_VALUES:], nc.scalar.copy, 1)
         third, opposite = multiply(0, 2), multiply(0, 3)
+        regroup(turned_w[0], w_values[:, :PAIR_VALUES], nc.vector.tensor_copy)
         regroup(turned_w[1], w_values[:, PAIR_VALUES:], nc.scalar.copy)
         quantise(next_values[:], x_codes, x_scales, PAIRS, PAIRS)
         fold(0, third)

@@ -233,13 +233,15 @@ def tile_conceptembedmodel_pa_kernel(tc, x, conv_w, conv_b, out):
         v, above, below, grown, result = finish_tiles
 
         def finish_first_half():
-            cols = columns(0)
-            nc.gpsimd.tensor_tensor(
-                out=v[:, cols], in0=best[:, cols], in1=bias[:, cols], op=ALU.add
-            )
-            nc.scalar.activation(out=below[:, cols], in_=v[:, cols], func=ACT.Relu, scale=-1.0)
-            nc.scalar.activation(out=above[:, cols], in_=v[:, cols], func=ACT.Relu)
-            nc.scalar.activation(out=grown[:, cols], in_=below[:, cols], func=ACT.Exp, scale=-1.0)
+            pieces = [slice(0, HALF // 2), slice(HALF // 2, HALF)]
+            for cols in pieces:
+                nc.gpsimd.tensor_tensor(
+                    out=v[:, cols], in0=best[:, cols], in1=bias[:, cols], op=ALU.add
+                )
+                nc.scalar.activation(out=below[:, cols], in_=v[:, cols], func=ACT.Relu, scale=-1.0)
+                nc.scalar.activation(out=above[:, cols], in_=v[:, cols], func=ACT.Relu)
+            for cols in pieces:
+                nc.scalar.activation(out=grown[:, cols], in_=below[:, cols], func=ACT.Exp, scale=-1.0)
 
         def store(cols):
             nc.vector.scalar_tensor_tensor(
@@ -348,10 +350,10 @@ def tile_conceptembedmodel_pa_kernel(tc, x, conv_w, conv_b, out):
         join(1, last - 1, last, base, gain)
         fold(0, multiply(0, last * GROUP + 1))
         fold(1, multiply(1, (last - 1) * GROUP + 1))
-        fold(0, larger[:, place(0, last - 1)])
-        fold(1, larger[:, place(1, last - 1)])
         fold(0, multiply(0, last * GROUP + 2), PIECES)
+        fold(1, larger[:, place(1, last - 1)])
         fold(0, multiply(0, last * GROUP + 3), PIECES)
+        fold(0, larger[:, place(0, last - 1)], PIECES)
         add_joined([1], last, base, gain)
         finish_first_half()
         for l in range(GROUP):

from contextlib import ExitStack

import concourse.mybir as mybir
from concourse.masks import make_identity

F32 = mybir.dt.float32
BF16 = mybir.dt.bfloat16
U32 = mybir.dt.uint32
U8 = mybir.dt.uint8
I32 = mybir.dt.int32
FP8X4 = mybir.dt.float8_e4m3fn_x4
ALU = mybir.AluOpType
ACT = mybir.ActivationFunctionType

P = 128
SEQS, POSITIONS, FEATURES, CHANNELS = 128, 32, 512, 1024
WORDS = FEATURES // 2
PAIR = 2
PAIR_COLS = PAIR * P
PAIR_VALUES = PAIR_COLS * 4
HALF = 512
GROUP = 4
GROUPS = POSITIONS // GROUP
PAIRS = GROUP // PAIR
W_PAIRS = HALF // PAIR_COLS
WARM_UP = 5
PIECES = 2

FLOPS = 2 * SEQS * POSITIONS * FEATURES * CHANNELS


def tile_conceptembedmodel_pa_kernel(tc, x, conv_w, conv_b, out):
    nc = tc.nc
    with ExitStack() as ctx:
        keep = ctx.enter_context(tc.tile_pool(name="keep", bufs=1))
        stage = ctx.enter_context(tc.tile_pool(name="stage", bufs=4))
        parts = ctx.enter_context(tc.tile_pool(name="parts", bufs=2))
        finish_pool = ctx.enter_context(tc.tile_pool(name="finish", bufs=1))
        turn_pool = ctx.enter_context(tc.psum_pool(name="turn", bufs=2))
        z_pool = ctx.enter_context(tc.psum_pool(name="z", bufs=6))
        ctx.enter_context(tc.manual_schedule())

        ident = keep.tile([P, P], F32)
        make_identity(nc, ident[:])

        zeros = keep.tile([P, HALF], BF16)
        nc.vector.memset(zeros[:].bitcast(I32), 0)

        unread = z_pool.tile([P, HALF], F32, tag="z")

        def idle_matmul():
            nc.tensor.matmul(out=unread[:], lhsT=zeros[:, :P], rhs=zeros[:], start=True, stop=True)

        for i in range(WARM_UP):
            idle_matmul()

        x_raw = keep.tile([P, POSITIONS * FEATURES], BF16)
        w_raw = keep.tile([P, (CHANNELS // P) * FEATURES], BF16)
        bias = keep.tile([P, CHANNELS], BF16)
        raw_cols = PAIR * FEATURES

        def load_w_pair(j):
            nc.sync.dma_start(
                out=w_raw[:, j * raw_cols : (j + 1) * raw_cols].rearrange(
                    "r (s f) -> r s f", s=PAIR
                ),
                in_=conv_w[j * PAIR_COLS : (j + 1) * PAIR_COLS, :].rearrange(
                    "(s r) f -> r s f", s=PAIR
                ),
            )

        def load_x_pair(j):
            nc.sync.dma_start(
                out=x_raw[:, j * raw_cols : (j + 1) * raw_cols],
                in_=x[:, j * PAIR : (j + 1) * PAIR, :].rearrange("b l f -> b (l f)"),
            )

        def load_x_group(g):
            for j in range(g * PAIRS, (g + 1) * PAIRS):
                load_x_pair(j)

        load_w_pair(0)
        load_x_pair(0)
        load_w_pair(1)
        load_x_pair(1)
        load_x_group(1)
        load_w_pair(2)
        load_w_pair(3)
        for g in range(2, GROUPS):
            load_x_group(g)
        nc.sync.dma_start(out=bias[:], in_=conv_b.partition_broadcast(P))

        x_codes = keep.tile([P, POSITIONS * P], U32, align_bytes=64)
        x_scales = keep.tile([P, POSITIONS * P], U8, align_bytes=64)
        w_codes = keep.tile([P, CHANNELS], U32, align_bytes=64)
        w_scales = keep.tile([P, CHANNELS], U8, align_bytes=64)
        x_words = x_raw[:].bitcast(F32)
        w_words = w_raw[:].bitcast(F32)

        def turn_pair(words, j, pool, tag):
            turned = pool.tile([P, PAIR, 2, P], F32, tag=tag)
            for s in range(PAIR):
                for u in range(2):
                    first = (j * PAIR + s) * WORDS
                    nc.tensor.transpose(
                        turned[:, s, u, :], words[:, first + u : first + WORDS : 2], ident[:]
                    )
            return turned

        def new_values(pairs):
            values = stage.tile([P, pairs * PAIR_VALUES], BF16, tag="v%d" % pairs, align_bytes=64)
            return values

        def regroup(turned, values, copy, flip=None):
            if flip is None:
                copy(
                    out=values.bitcast(F32).rearrange("p (s r u) -> p s r u", s=PAIR, u=2),
                    in_=turned[:].rearrange("p s u r -> p s r u"),
                )
                return
            for s in range(PAIR):
                block = values[:, s * P * 4 : (s + 1) * P * 4]
                if s == flip:
                    nc.scalar.activation(
                        out=block.rearrange("p (r u e) -> p r u e", u=2, e=2),
                        in_=turned[:, s, :, :]
                        .rearrange("p u r -> p (u r)")
                        .bitcast(BF16)
                        .rearrange("p (u r e) -> p r u e", u=2, e=2),
                        func=ACT.Copy,
                        scale=-1.0,
                    )
                else:
                    copy(
                        out=block.bitcast(F32).rearrange("p (r u) -> p r u", u=2),
                        in_=turned[:, s, :, :].rearrange("p u r -> p r u"),
                    )

        def quantise(values, codes, scales, j, pairs):
            cols = slice(j * PAIR_COLS, (j + pairs) * PAIR_COLS)
            nc.vector.quantize_mx(
                out=codes[:, cols].bitcast(FP8X4), scales=scales[:, cols], in_=values
            )

        def prepare_group(g):
            turned = [turn_pair(x_words, g * PAIRS + k, turn_pool, "turn") for k in range(PAIRS)]
            values = new_values(PAIRS)
            regroup(turned[0], values[:, :PAIR_VALUES], nc.scalar.copy)
            regroup(turned[1], values[:, PAIR_VALUES:], nc.scalar.copy, 1 if g < GROUPS - 1 else None)
            return values

        def multiply(h, *positions, part=slice(0, HALF)):
            z = z_pool.tile([P, HALF], F32)
            chans = slice(h * HALF + part.start, h * HALF + part.stop)
            for k, l in enumerate(positions):
                seqs = slice(l * P, (l + 1) * P)
                nc.tensor.matmul_mx(
                    out=z[:, part],
                    lhsT=x_codes[:, seqs].bitcast(FP8X4),
                    lhsT_scale=x_scales[:, seqs],
                    rhs=w_codes[:, chans].bitcast(FP8X4),
                    rhs_scale=w_scales[:, chans],
                    start=(k == 0),
                    stop=(k == len(positions) - 1),
                )
            return z

        best = keep.tile([P, CHANNELS], F32)
        larger = keep.tile([P, 3 * HALF], F32)

        def columns(h):
            return slice(h * HALF, (h + 1) * HALF)

        def fold(h, z, pieces=1):
            width = HALF // pieces
            for c in range(pieces):
                cols = slice(h * HALF + c * width, h * HALF + (c + 1) * width)
                nc.vector.tensor_tensor(
                    out=best[:, cols],
                    in0=z[:, c * width : (c + 1) * width],
                    in1=best[:, cols],
                    op=ALU.max,
                )

        def start(h, z, part=slice(0, HALF)):
            cols = slice(h * HALF + part.start, h * HALF + part.stop)
            nc.scalar.copy(out=best[:, cols], in_=z[:, part])

        def fold_opposite(h, z):
            cols = columns(h)
            nc.vector.scalar_tensor_tensor(
                out=best[:, cols],
                in0=z[:],
                scalar=-1.0,
                in1=best[:, cols],
                op0=ALU.mult,
                op1=ALU.max,
            )

        def place(h, i):
            third = 1 if h == 0 else 2 * (i % 2)
            return slice(third * HALF, (third + 1) * HALF)

        def inside(h, i):
            first = place(h, i).start - (i % 2) * HALF
            return slice(first, first + HALF)

        def new_parts():
            base = parts.tile([P, CHANNELS], F32)
            gain = parts.tile([P, CHANNELS], F32)
            return base, gain

        def join(h, g, i, base, gain):
            c, d = g * GROUP + 2, g * GROUP + 3
            cols = inside(h, i)
            nc.scalar.copy(out=base[:, cols], in_=multiply(h, c)[:])
            nc.scalar.activation(
                out=gain[:, cols], in_=multiply(h, c, d)[:], func=ACT.Relu, scale=-1.0
            )

        def add_joined(halves, i, base, gain):
            starts = [inside(h, i).start for h in halves]
            cols = slice(min(starts), max(starts) + HALF)
            shift = (i % 2) * HALF
            nc.gpsimd.tensor_tensor(
                out=larger[:, cols.start + shift : cols.stop + shift],
                in0=base[:, cols],
                in1=gain[:, cols],
                op=ALU.add,
            )

        finish_tiles = [finish_pool.tile([P, CHANNELS], F32, name="f%d" % k) for k in range(5)]
        v, above, below, grown, result = finish_tiles

        def finish_first_half():
            pieces = [slice(0, HALF // 2), slice(HALF // 2, HALF)]
            for cols in pieces:
                nc.gpsimd.tensor_tensor(
                    out=v[:, cols], in0=best[:, cols], in1=bias[:, cols], op=ALU.add
                )
                nc.scalar.activation(out=below[:, cols], in_=v[:, cols], func=ACT.Relu, scale=-1.0)
                nc.scalar.activation(out=above[:, cols], in_=v[:, cols], func=ACT.Relu)
            for cols in pieces:
                nc.scalar.activation(out=grown[:, cols], in_=below[:, cols], func=ACT.Exp, scale=-1.0)

        def store(cols):
            nc.vector.scalar_tensor_tensor(
                out=result[:, cols],
                in0=grown[:, cols],
                scalar=-1.0,
                in1=above[:, cols],
                op0=ALU.add,
                op1=ALU.add,
            )
            nc.sync.dma_start(out=out[:, cols], in_=result[:, cols])

        def finish_second_half():
            width = HALF // PIECES
            pieces = [slice(HALF + c * width, HALF + (c + 1) * width) for c in range(PIECES)]
            for cols in pieces:
                nc.vector.tensor_tensor(
                    out=v[:, cols], in0=best[:, cols], in1=bias[:, cols], op=ALU.add
                )
            for cols in pieces:
                nc.vector.tensor_scalar(
                    out=below[:, cols], in0=v[:, cols], scalar1=0.0, scalar2=None, op0=ALU.min
                )
                nc.scalar.activation(out=grown[:, cols], in_=below[:, cols], func=ACT.Exp)
            cols = columns(1)
            nc.vector.tensor_scalar(
                out=above[:, cols], in0=v[:, cols], scalar1=0.0, scalar2=None, op0=ALU.max
            )
            store(columns(0))
            for cols in pieces:
                store(cols)

        parts_w = [slice(j * PAIR_COLS, (j + 1) * PAIR_COLS) for j in range(W_PAIRS)]
        w_values = [new_values(1) for j in range(W_PAIRS)]
        x_values = [new_values(1) for j in range(PAIRS)]
        next_values = new_values(PAIRS)
        turned_w = [turn_pair(w_words, 0, turn_pool, "turn")]
        turned_x = [turn_pair(x_words, 0, z_pool, "z")]
        turned_w.append(turn_pair(w_words, 1, turn_pool, "turn"))
        turned_x.append(turn_pair(x_words, 1, z_pool, "z"))
        idle_matmul()
        regroup(turned_w[0], w_values[0][:], nc.scalar.copy)
        regroup(turned_x[0], x_values[0][:], nc.vector.tensor_copy)
        regroup(turned_w[1], w_values[1][:], nc.scalar.copy)
        regroup(turned_x[1], x_values[1][:], nc.scalar.copy, 1)
        quantise(w_values[0][:], w_codes, w_scales, 0, 1)
        quantise(x_values[0][:], x_codes, x_scales, 0, 1)
        turned_x = [turn_pair(x_words, PAIRS, turn_pool, "turn")]
        start(0, multiply(0, 0, part=parts_w[0]), parts_w[0])
        second = [multiply(0, 1, part=parts_w[0])]
        quantise(w_values[1][:], w_codes, w_scales, 1, 1)
        regroup(turned_x[0], next_values[:, :PAIR_VALUES], nc.vector.tensor_copy)
        start(0, multiply(0, 0, part=parts_w[1]), parts_w[1])
        second.append(multiply(0, 1, part=parts_w[1]))
        turned_x.append(turn_pair(x_words, PAIRS + 1, turn_pool, "turn"))
        quantise(x_values[1][:], x_codes, x_scales, 1, 1)
        for k in range(W_PAIRS):
            cols = parts_w[k]
            nc.vector.tensor_tensor(
                out=best[:, cols], in0=second[k][:, cols], in1=best[:, cols], op=ALU.max
            )
        turned_w = [turn_pair(w_words, W_PAIRS + j, z_pool, "z") for j in range(W_PAIRS)]
        w_values = new_values(W_PAIRS)
        regroup(turned_x[1], next_values[:, PAIR_VALUES:], nc.scalar.copy, 1)
        third, opposite = multiply(0, 2), multiply(0, 3)
        regroup(turned_w[0], w_values[:, :PAIR_VALUES], nc.vector.tensor_copy)
        regroup(turned_w[1], w_values[:, PAIR_VALUES:], nc.scalar.copy)
        quantise(next_values[:], x_codes, x_scales, PAIRS, PAIRS)
        fold(0, third)
        quantise(w_values[:], w_codes, w_scales, W_PAIRS, W_PAIRS)
        fold_opposite(0, opposite)

        coming = prepare_group(2)
        fold(0, multiply(0, GROUP))
        start(1, multiply(1, 0))
        base, gain = new_parts()
        join(0, 1, 1, base, gain)
        waiting = [0]
        fold(1, multiply(1, 1))
        quantise(coming[:], x_codes, x_scales, 2 * PAIRS, PAIRS)
        fold_opposite(1, multiply(1, 3))
        fold(0, multiply(0, GROUP + 1))
        fold(1, multiply(1, 2))

        for i in range(2, GROUPS - 1):
            coming = prepare_group(i + 1)
            add_joined(waiting, i - 1, base, gain)
            base, gain = new_parts()
            work = [(0, i), (1, i - 1)]
            for h, g in work:
                fold(h, multiply(h, g * GROUP))
            for h, g in work:
                join(h, g, i, base, gain)
            quantise(coming[:], x_codes, x_scales, (i + 1) * PAIRS, PAIRS)
            for h in waiting:
                fold(h, larger[:, place(h, i - 1)])
            for h, g in work:
                fold(h, multiply(h, g * GROUP + 1))
            waiting = [0, 1]

        last = GROUPS - 1
        add_joined(waiting, last - 1, base, gain)
        base, gain = new_parts()
        fold(0, multiply(0, last * GROUP))
        fold(1, multiply(1, (last - 1) * GROUP))
        join(1, last - 1, last, base, gain)
        fold(0, multiply(0, last * GROUP + 1))
        fold(1, multiply(1, (last - 1) * GROUP + 1))
        fold(0, multiply(0, last * GROUP + 2), PIECES)
        fold(1, larger[:, place(1, last - 1)])
        fold(0, multiply(0, last * GROUP + 3), PIECES)
        fold(0, larger[:, place(0, last - 1)], PIECES)
        add_joined([1], last, base, gain)
        finish_first_half()
        for l in range(GROUP):
            fold(1, multiply(1, last * GROUP + l), PIECES)
        fold(1, larger[:, place(1, last)], PIECES)
        finish_second_half()
